import numpy as np
import ml_dtypes


def mxq(x, axis, fmt="e4m3"):
    dtype, down = {"e4m3": (ml_dtypes.float8_e4m3fn, 7), "e5m2": (ml_dtypes.float8_e5m2, 14)}[fmt]
    v = np.moveaxis(np.asarray(x, np.float32).astype(ml_dtypes.bfloat16).astype(np.float64), axis, -1)
    blocks = v.reshape(v.shape[:-1] + (-1, 32))
    amax = np.abs(blocks).max(-1, keepdims=True)
    byte = np.maximum(np.where(amax > 0, np.frexp(amax)[1] - 1 + 127, 0) - down, 1)
    scale = np.exp2(byte - 127.0)
    codes = (blocks / scale).astype(np.float32).astype(dtype).astype(np.float64)
    return np.moveaxis((codes * scale).reshape(v.shape), -1, axis)


WIDE = False


def mx_kscale(k):
    if not WIDE:
        return np.ones(k)
    levels = np.array([10, -10, 5, -5, 0])
    a = np.random.permutation(np.resize(levels, k // 512 * 4)).reshape(k // 512, 4)
    idx = np.arange(k)
    return np.exp2(a[idx // 512, idx % 128 // 32])


BF16 = ml_dtypes.bfloat16


def bf(x):
    return np.asarray(x, np.float32).astype(BF16)


def f64(x):
    return np.asarray(x).astype(np.float64)


B, N, D, H, DH, GD = 2, 1024, 1024, 8, 128, 128
INNER = H * DH
LN_EPS = 1e-5


def silu(v):
    return v / (1.0 + np.exp(-v))


def sigmoid(v):
    return 1.0 / (1.0 + np.exp(-v))


def setup_inputs():
    t = mx_kscale(INNER)
    theta = (10000.0 ** (-2.0 / INNER * np.arange(INNER)) * (1.0 + 0.1 * np.random.standard_normal(INNER))).reshape(H, 1, DH)
    ang = theta * np.arange(N).reshape(1, N, 1)
    tab = np.concatenate([np.cos(ang), np.sin(ang)], axis=-1)
    qs = silu(np.random.standard_normal((B, H, N, DH)))
    mu, m2 = qs.mean(), (qs ** 2).mean()
    kv_mean = mu * mu * tab.sum(1)
    kv_spread = np.sqrt((m2 * m2 - mu ** 4) * (tab ** 2).sum(1))
    kv = (kv_mean[None, :, :, None] + kv_spread[None, :, :, None] * np.random.standard_normal((B, H, 2 * DH, DH))) / np.sqrt(2 * DH)
    return {"q_rot": bf(np.concatenate([qs, qs], axis=-1) * tab[None] / np.sqrt(2 * DH)),
            "kv": bf(kv),
            "g_low": bf(np.random.standard_normal((B, N, GD))),
            "w_g2": bf(np.random.standard_normal((GD, INNER)) / np.sqrt(GD)),
            "ln_gamma": bf((1.0 + 0.1 * np.random.standard_normal(INNER)) * t),
            "ln_beta": bf(0.1 * np.random.standard_normal(INNER) * t),
            "w_out": bf(np.random.standard_normal((INNER, D)) / np.sqrt(INNER) / t[:, None]),
            "b_out": bf(0.1 * np.random.standard_normal(D))}


def reference(q_rot, kv, g_low, w_g2, ln_gamma, ln_beta, w_out, b_out):
    o = f64(q_rot) @ f64(kv)
    o = o.transpose(0, 2, 1, 3).reshape(B, N, INNER)
    mu = o.mean(-1, keepdims=True)
    var = ((o - mu) ** 2).mean(-1, keepdims=True)
    y = (o - mu) / np.sqrt(var + LN_EPS) * f64(ln_gamma) + f64(ln_beta)
    gate = sigmoid(f64(g_low) @ f64(w_g2))
    h = y * gate
    return (mxq(h, 2, "e4m3") @ mxq(f64(w_out), 0, "e4m3")) + f64(b_out)

@@ -1,0 +1,347 @@
+from contextlib import ExitStack
+
+import concourse.mybir as mybir
+from concourse.masks import make_identity
+
+F32 = mybir.dt.float32
+BF16 = mybir.dt.bfloat16
+U32 = mybir.dt.uint32
+U8 = mybir.dt.uint8
+FP8X4 = mybir.dt.float8_e4m3fn_x4
+ACT = mybir.ActivationFunctionType
+ALU = mybir.AluOpType
+
+P = 128
+BATCH, SEQ, HEADS, HEAD_DIM = 2, 1024, 8, 128
+INNER = HEADS * HEAD_DIM
+D_OUT = 1024
+LN_EPS = 1e-5
+
+PACK = 4
+K_PASS = P * PACK
+PASSES = INNER // K_PASS
+CHUNKS = INNER // P
+BANK = 512
+ROW_TILES = 4
+BLOCK = ROW_TILES * P
+BLOCKS_PER_SEQ = SEQ // BLOCK
+BLOCKS = BATCH * BLOCKS_PER_SEQ
+HEADS_PER_BANK = BANK // HEAD_DIM
+O_BANKS = INNER // BANK
+OUT_BANKS = D_OUT // BANK
+ROWS = BLOCKS * ROW_TILES
+ALL_PASSES = BLOCKS * PASSES
+QUANT_TILES = 2
+QUANTS = ROW_TILES // QUANT_TILES
+
+GATE_LEAD = 3
+Q_LEAD = 1
+NORM_LAG = 1
+FLIP_LAG = ROW_TILES + NORM_LAG
+GROUP_LAG = FLIP_LAG + 2
+PROJECT_LAG = GROUP_LAG + PASSES * QUANTS - 1
+W_TICK = 4
+
+FLOPS = 2 * BATCH * SEQ * (HEADS * 2 * HEAD_DIM * HEAD_DIM + HEAD_DIM * INNER + INNER * D_OUT)
+
+
+def due(index, count):
+    return 0 <= index < count
+
+
+def tile_linearattention_pb_kernel(
+    tc, q_rot, kv, g_low, w_g2, ln_gamma, ln_beta, w_out, b_out, out
+):
+    nc = tc.nc
+    with ExitStack() as ctx:
+        const = ctx.enter_context(tc.tile_pool(name="const", bufs=1))
+        q_pool = ctx.enter_context(tc.tile_pool(name="q", bufs=2 * O_BANKS))
+        qt_pool = ctx.enter_context(tc.tile_pool(name="qt", bufs=3))
+        block_pool = ctx.enter_context(tc.tile_pool(name="block", bufs=2))
+        gate_pool = ctx.enter_context(tc.tile_pool(name="gate", bufs=6))
+        mx_pool = ctx.enter_context(tc.tile_pool(name="mx", bufs=2 * PASSES * QUANTS))
+        stat_pool = ctx.enter_context(tc.tile_pool(name="stat", bufs=4))
+        out_pool = ctx.enter_context(tc.tile_pool(name="outs", bufs=4))
+        ps_short = ctx.enter_context(tc.psum_pool(name="ps_short", bufs=3))
+        ps_o = ctx.enter_context(tc.psum_pool(name="ps_o", bufs=3))
+        ps_acc = ctx.enter_context(tc.psum_pool(name="ps_acc", bufs=2))
+        ctx.enter_context(tc.manual_schedule())
+
+        ident_bf = const.tile([P, P], BF16)
+        make_identity(nc, ident_bf[:])
+        ident_f32 = const.tile([P, P], F32)
+        make_identity(nc, ident_f32[:])
+        neg_half = const.tile([P, 1], F32)
+        nc.vector.memset(neg_half[:], -0.5)
+
+        g_sb = const.tile([P, BLOCKS, ROW_TILES, HEAD_DIM], BF16)
+        nc.sync.dma_start(
+            out=g_sb[:].rearrange("p s j g -> p s (j g)"),
+            in_=g_low.rearrange("b (s p j) g -> p (b s) (j g)", p=P, j=ROW_TILES),
+        )
+        wg_sb = const.tile([P, INNER], BF16)
+        nc.sync.dma_start(out=wg_sb[:], in_=w_g2)
+
+        gb_rows = const.tile([P, P], BF16)
+        nc.vector.memset(gb_rows[:], 0.0)
+        nc.sync.dma_start(out=gb_rows[0:CHUNKS, :], in_=ln_gamma.rearrange("(c p) -> c p", p=P))
+        nc.sync.dma_start(
+            out=gb_rows[CHUNKS : 2 * CHUNKS, :], in_=ln_beta.rearrange("(c p) -> c p", p=P)
+        )
+
+        kv_sb = const.tile([P, BATCH * HEADS, 2, HEAD_DIM], BF16)
+        kv_view = kv.rearrange("b h (w e) d -> w (b h) (e d)", e=2)
+
+        def load_kv(b):
+            heads = slice(b * HEADS, (b + 1) * HEADS)
+            nc.sync.dma_start(
+                out=kv_sb[:, heads, :, :].rearrange("w h e d -> w h (e d)"), in_=kv_view[:, heads, :]
+            )
+
+        q_tiles = {}
+
+        def load_q(blk):
+            b, s = divmod(blk, BLOCKS_PER_SEQ)
+            rows = slice(s * BLOCK, (s + 1) * BLOCK)
+            for half in range(O_BANKS):
+                heads = slice(half * HEADS_PER_BANK, (half + 1) * HEADS_PER_BANK)
+                q_sb = q_pool.tile([P, HEADS_PER_BANK, ROW_TILES, 2 * HEAD_DIM], BF16)
+                nc.sync.dma_start(
+                    out=q_sb[:].rearrange("p h j k -> p h (j k)"),
+                    in_=q_rot[b, heads, rows, :].rearrange("h (p j) k -> p h (j k)", j=ROW_TILES),
+                )
+                q_tiles[(blk, half)] = q_sb
+
+        load_q(0)
+        load_kv(0)
+        load_q(1)
+        w_sb = const.tile([P, CHUNKS, D_OUT], BF16)
+        w_view = w_out.rearrange("(c p) n -> p c n", p=P)
+        for g in range(PASSES):
+            chunks = slice(g * PACK, (g + 1) * PACK)
+            nc.sync.dma_start(out=w_sb[:, chunks, :], in_=w_view[:, chunks, :])
+        load_kv(1)
+        bias_bf = const.tile([P, D_OUT], BF16)
+        nc.sync.dma_start(out=bias_bf[:], in_=b_out.partition_broadcast(P))
+
+        g_t = const.tile([P, BLOCKS, ROW_TILES, P], BF16)
+        for blk in range(BLOCKS):
+            gt_ps = ps_short.tile([P, ROW_TILES, P], BF16, tag="short")
+            for j in range(ROW_TILES):
+                nc.tensor.transpose(gt_ps[:, j, :], g_sb[:, blk, j, :], ident_bf[:])
+            nc.vector.tensor_copy(out=g_t[:, blk, :, :], in_=gt_ps[:])
+        gb_ps = ps_short.tile([P, P], BF16, tag="short")
+        nc.tensor.transpose(gb_ps[:], gb_rows[:], ident_bf[:])
+        gamma_beta = const.tile([P, 2 * CHUNKS], F32)
+        nc.vector.tensor_copy(out=gamma_beta[:], in_=gb_ps[:, 0 : 2 * CHUNKS])
+
+        w_codes = const.tile([P, PASSES, D_OUT], U32, align_bytes=64)
+        w_scales = const.tile([P, PASSES, D_OUT], U8, align_bytes=64)
+        w_grouped = {}
+
+        def weight_piece(i):
+            g, bank = divmod(i, OUT_BANKS)
+            cols = slice(bank * BANK, (bank + 1) * BANK)
+            if bank == 0:
+                grouped = const.tile([P, D_OUT, PACK], BF16, align_bytes=64, tag="w_grouped")
+                w_grouped[g] = grouped
+            nc.vector.tensor_copy(
+                out=w_grouped[g][:, cols, :].rearrange("p (c i) t -> p c t i", i=4),
+                in_=w_sb[:, g * PACK : (g + 1) * PACK, cols].rearrange("p t (c i) -> p c t i", i=4),
+            )
+            if bank == OUT_BANKS - 1:
+                nc.vector.quantize_mx(
+                    out=w_codes[:, g, :].bitcast(FP8X4),
+                    scales=w_scales[:, g, :],
+                    in_=w_grouped[g][:].rearrange("p n t -> p (n t)"),
+                )
+
+        gates = {}
+
+        def gate_piece(v):
+            pair, part = divmod(v, QUANTS)
+            blk, g = divmod(pair, PASSES)
+            if part == 0:
+                gate = gate_pool.tile([P, ROW_TILES, P, PACK], F32)
+                gates[pair] = gate
+            for j in range(part * QUANT_TILES, (part + 1) * QUANT_TILES):
+                u_ps = ps_short.tile([P, PACK, P], F32, tag="short")
+                for t in range(PACK):
+                    c = g * PACK + t
+                    nc.tensor.matmul(
+                        out=u_ps[:, t, :],
+                        lhsT=wg_sb[:, c * P : (c + 1) * P],
+                        rhs=g_t[:, blk, j, :],
+                        start=True,
+                        stop=True,
+                    )
+                nc.scalar.activation(
+                    out=gates[pair][:, j, :, :],
+                    in_=u_ps[:].rearrange("p t n -> p n t"),
+                    func=ACT.Sigmoid,
+                )
+
+        q_t = {}
+
+        def q_piece(r, half):
+            blk, j = divmod(r, ROW_TILES)
+            if half == 0:
+                words = qt_pool.tile([P, HEADS, P], F32)
+                q_t[r] = words
+            tq_ps = ps_short.tile([P, HEADS_PER_BANK, P], F32, tag="short")
+            for hh in range(HEADS_PER_BANK):
+                nc.tensor.transpose(
+                    tq_ps[:, hh, :], q_tiles[(blk, half)][:, hh, j, :].bitcast(F32), ident_f32[:]
+                )
+            heads = slice(half * HEADS_PER_BANK, (half + 1) * HEADS_PER_BANK)
+            nc.scalar.copy(out=q_t[r][:, heads, :], in_=tq_ps[:])
+
+        o_banks = {}
+        norm_terms = {}
+
+        def heads_piece(r):
+            b = r // (ROW_TILES * BLOCKS_PER_SEQ)
+            stats = stat_pool.tile([P, O_BANKS, 6], F32)
+            o_banks[r] = []
+            for half in range(O_BANKS):
+                o_ps = ps_o.tile([P, HEADS_PER_BANK, HEAD_DIM], F32)
+                for hh in range(HEADS_PER_BANK):
+                    h = half * HEADS_PER_BANK + hh
+                    pairs = q_t[r][:, h, :].bitcast(BF16).rearrange("w (n e) -> w n e", e=2)
+                    for e in range(2):
+                        nc.tensor.matmul(
+                            out=o_ps[:, hh, :],
+                            lhsT=pairs[:, :, e],
+                            rhs=kv_sb[:, b * HEADS + h, e, :],
+                            start=(e == 0),
+                            stop=(e == 1),
+                        )
+                nc.vector.bn_stats(out=stats[:, half, :], in_=o_ps[:].rearrange("p h d -> p (h d)"))
+                o_banks[r].append(o_ps)
+            mean_var = stat_pool.tile([P, 2], F32)
+            nc.vector.bn_aggr(out=mean_var[:], in_=stats[:].rearrange("p a s -> p (a s)"))
+            var_eps = stat_pool.tile([P, 1], F32)
+            nc.vector.tensor_scalar(
+                out=var_eps[:], in0=mean_var[:, 1:2], scalar1=LN_EPS, scalar2=None, op0=ALU.add
+            )
+            neg_mean = stat_pool.tile([P, 1], F32)
+            nc.vector.tensor_scalar(
+                out=neg_mean[:], in0=mean_var[:, 0:1], scalar1=-1.0, scalar2=None, op0=ALU.mult
+            )
+            rstd = stat_pool.tile([P, 1], F32)
+            nc.gpsimd.tensor_tensor(out=rstd[:], in0=var_eps[:], in1=neg_half[:], op=ALU.pow)
+            shift = stat_pool.tile([P, 1], F32)
+            nc.gpsimd.tensor_tensor(out=shift[:], in0=neg_mean[:], in1=rstd[:], op=ALU.mult)
+            norm_terms[r] = (rstd, shift)
+
+        x_hat = {}
+
+        def norm_piece(r):
+            blk, j = divmod(r, ROW_TILES)
+            if j == 0:
+                normed = block_pool.tile([P, ROW_TILES, INNER], F32)
+                x_hat[blk] = normed
+            rstd, shift = norm_terms[r]
+            for half in range(O_BANKS):
+                nc.scalar.activation(
+                    out=x_hat[blk][:, j, half * BANK : (half + 1) * BANK],
+                    in_=o_banks[r][half][:].rearrange("p h d -> p (h d)"),
+                    func=ACT.Identity,
+                    scale=rstd[:, 0:1],
+                    bias=shift[:, 0:1],
+                )
+
+        y_t = {}
+
+        def flip_piece(u):
+            pair, part = divmod(u, 2)
+            blk, g = divmod(pair, PASSES)
+            if part == 0:
+                scaled = block_pool.tile([P, PACK, ROW_TILES, P], F32)
+                y_t[pair] = scaled
+            for t in (2 * part, 2 * part + 1):
+                c = g * PACK + t
+                xt_ps = ps_short.tile([P, ROW_TILES, P], F32, tag="short")
+                for j in range(ROW_TILES):
+                    nc.tensor.transpose(
+                        xt_ps[:, j, :], x_hat[blk][:, j, c * P : (c + 1) * P], ident_f32[:]
+                    )
+                nc.scalar.activation(
+                    out=y_t[pair][:, t, :, :],
+                    in_=xt_ps[:],
+                    func=ACT.Identity,
+                    scale=gamma_beta[:, c : c + 1],
+                    bias=gamma_beta[:, CHUNKS + c : CHUNKS + c + 1],
+                )
+
+        h_mx = {}
+
+        def group_piece(i):
+            pair, part = divmod(i, QUANTS)
+            tiles = slice(part * QUANT_TILES, (part + 1) * QUANT_TILES)
+            h_grouped = block_pool.tile([P, QUANT_TILES * P, PACK], BF16, align_bytes=64)
+            nc.vector.tensor_tensor(
+                out=h_grouped[:],
+                in0=y_t[pair][:, :, tiles, :].rearrange("p t j n -> p (j n) t"),
+                in1=gates[pair][:, tiles, :, :].rearrange("p j n t -> p (j n) t"),
+                op=ALU.mult,
+            )
+            h_codes = mx_pool.tile([P, QUANT_TILES * P], U32, align_bytes=64)
+            h_scales = mx_pool.tile([P, QUANT_TILES * P], U8, align_bytes=64)
+            nc.vector.quantize_mx(
+                out=h_codes[:].bitcast(FP8X4),
+                scales=h_scales[:],
+                in_=h_grouped[:].rearrange("p m t -> p (m t)"),
+            )
+            h_mx[(pair, part)] = (h_codes, h_scales)
+
+        def project_piece(r):
+            blk, j = divmod(r, ROW_TILES)
+            b, s = divmod(blk, BLOCKS_PER_SEQ)
+            part, jj = divmod(j, QUANT_TILES)
+            rows = slice(jj * P, (jj + 1) * P)
+            result = out_pool.tile([P, D_OUT], F32)
+            for bank in range(OUT_BANKS):
+                cols = slice(bank * BANK, (bank + 1) * BANK)
+                acc = ps_acc.tile([P, BANK], F32)
+                for g in range(PASSES):
+                    h_codes, h_scales = h_mx[(blk * PASSES + g, part)]
+                    nc.tensor.matmul_mx(
+                        out=acc[:],
+                        lhsT=h_codes[:, rows].bitcast(FP8X4),
+                        lhsT_scale=h_scales[:, rows],
+                        rhs=w_codes[:, g, cols].bitcast(FP8X4),
+                        rhs_scale=w_scales[:, g, cols],
+                        start=(g == 0),
+                        stop=(g == PASSES - 1),
+                    )
+                nc.vector.tensor_tensor(
+                    out=result[:, cols], in0=acc[:], in1=bias_bf[:, cols], op=ALU.add
+                )
+            out_rows = out[b, s * BLOCK : (s + 1) * BLOCK, :].rearrange(
+                "(p j) d -> p j d", j=ROW_TILES
+            )
+            nc.sync.dma_start(out=out_rows[:, j, :], in_=result[:])
+
+        for tick in range(-GATE_LEAD, ROWS + PROJECT_LAG):
+            if due(tick - NORM_LAG, ROWS):
+                norm_piece(tick - NORM_LAG)
+            if due(tick - FLIP_LAG, ROWS):
+                flip_piece(tick - FLIP_LAG)
+            if due(tick + Q_LEAD, ROWS):
+                q_piece(tick + Q_LEAD, 0)
+            if due(tick, ROWS):
+                heads_piece(tick)
+            if due(tick + Q_LEAD, ROWS):
+                q_piece(tick + Q_LEAD, 1)
+                blk, j = divmod(tick + Q_LEAD, ROW_TILES)
+                if j == ROW_TILES - 1 and blk + 2 < BLOCKS:
+                    load_q(blk + 2)
+            if due(tick + GATE_LEAD, ROWS):
+                gate_piece(tick + GATE_LEAD)
+            if due(tick - GROUP_LAG, ROWS):
+                group_piece(tick - GROUP_LAG)
+            if due(tick - W_TICK, PASSES * OUT_BANKS):
+                weight_piece(tick - W_TICK)
+            if due(tick - PROJECT_LAG, ROWS):
+                project_piece(tick - PROJECT_LAG)

@@ -45,10 +45,6 @@ W_TICK = 4
 FLOPS = 2 * BATCH * SEQ * (HEADS * 2 * HEAD_DIM * HEAD_DIM + HEAD_DIM * INNER + INNER * D_OUT)
 
 
-def due(index, count):
-    return 0 <= index < count
-
-
 def tile_linearattention_pb_kernel(
     tc, q_rot, kv, g_low, w_g2, ln_gamma, ln_beta, w_out, b_out, out
 ):
@@ -158,28 +154,25 @@ def tile_linearattention_pb_kernel(
 
         gates = {}
 
-        def gate_piece(v):
-            pair, part = divmod(v, QUANTS)
+        def gate_piece(v, step):
+            pair, j = divmod(2 * v + step, ROW_TILES)
             blk, g = divmod(pair, PASSES)
-            if part == 0:
+            if j == 0:
                 gate = gate_pool.tile([P, ROW_TILES, P, PACK], F32)
                 gates[pair] = gate
-            for j in range(part * QUANT_TILES, (part + 1) * QUANT_TILES):
-                u_ps = ps_short.tile([P, PACK, P], F32, tag="short")
-                for t in range(PACK):
-                    c = g * PACK + t
-                    nc.tensor.matmul(
-                        out=u_ps[:, t, :],
-                        lhsT=wg_sb[:, c * P : (c + 1) * P],
-                        rhs=g_t[:, blk, j, :],
-                        start=True,
-                        stop=True,
-                    )
-                nc.scalar.activation(
-                    out=gates[pair][:, j, :, :],
-                    in_=u_ps[:].rearrange("p t n -> p n t"),
-                    func=ACT.Sigmoid,
+            u_ps = ps_short.tile([P, PACK, P], F32, tag="short")
+            for t in range(PACK):
+                c = g * PACK + t
+                nc.tensor.matmul(
+                    out=u_ps[:, t, :],
+                    lhsT=wg_sb[:, c * P : (c + 1) * P],
+                    rhs=g_t[:, blk, j, :],
+                    start=True,
+                    stop=True,
                 )
+            nc.scalar.activation(
+                out=gates[pair][:, j, :, :], in_=u_ps[:].rearrange("p t n -> p n t"), func=ACT.Sigmoid
+            )
 
         q_t = {}
 
@@ -199,27 +192,37 @@ def tile_linearattention_pb_kernel(
         o_banks = {}
         norm_terms = {}
 
-        def heads_piece(r):
+        stats_of = {}
+
+        def heads_piece(r, quarter):
             b = r // (ROW_TILES * BLOCKS_PER_SEQ)
-            stats = stat_pool.tile([P, O_BANKS, 6], F32)
-            o_banks[r] = []
-            for half in range(O_BANKS):
+            half, second = divmod(quarter, 2)
+            if quarter == 0:
+                stats = stat_pool.tile([P, O_BANKS, 6], F32)
+                stats_of[r] = stats
+                o_banks[r] = []
+            if second == 0:
                 o_ps = ps_o.tile([P, HEADS_PER_BANK, HEAD_DIM], F32)
-                for hh in range(HEADS_PER_BANK):
-                    h = half * HEADS_PER_BANK + hh
-                    pairs = q_t[r][:, h, :].bitcast(BF16).rearrange("w (n e) -> w n e", e=2)
-                    for e in range(2):
-                        nc.tensor.matmul(
-                            out=o_ps[:, hh, :],
-                            lhsT=pairs[:, :, e],
-                            rhs=kv_sb[:, b * HEADS + h, e, :],
-                            start=(e == 0),
-                            stop=(e == 1),
-                        )
-                nc.vector.bn_stats(out=stats[:, half, :], in_=o_ps[:].rearrange("p h d -> p (h d)"))
                 o_banks[r].append(o_ps)
+            for hh in (2 * second, 2 * second + 1):
+                h = half * HEADS_PER_BANK + hh
+                pairs = q_t[r][:, h, :].bitcast(BF16).rearrange("w (n e) -> w n e", e=2)
+                for e in range(2):
+                    nc.tensor.matmul(
+                        out=o_banks[r][half][:, hh, :],
+                        lhsT=pairs[:, :, e],
+                        rhs=kv_sb[:, b * HEADS + h, e, :],
+                        start=(e == 0),
+                        stop=(e == 1),
+                    )
+            if second == 1:
+                nc.vector.bn_stats(
+                    out=stats_of[r][:, half, :], in_=o_banks[r][half][:].rearrange("p h d -> p (h d)")
+                )
+
+        def stats_piece(r):
             mean_var = stat_pool.tile([P, 2], F32)
-            nc.vector.bn_aggr(out=mean_var[:], in_=stats[:].rearrange("p a s -> p (a s)"))
+            nc.vector.bn_aggr(out=mean_var[:], in_=stats_of[r][:].rearrange("p a s -> p (a s)"))
             var_eps = stat_pool.tile([P, 1], F32)
             nc.vector.tensor_scalar(
                 out=var_eps[:], in0=mean_var[:, 1:2], scalar1=LN_EPS, scalar2=None, op0=ALU.add
@@ -236,43 +239,39 @@ def tile_linearattention_pb_kernel(
 
         x_hat = {}
 
-        def norm_piece(r):
+        def norm_piece(r, half):
             blk, j = divmod(r, ROW_TILES)
-            if j == 0:
+            if j == 0 and half == 0:
                 normed = block_pool.tile([P, ROW_TILES, INNER], F32)
                 x_hat[blk] = normed
             rstd, shift = norm_terms[r]
-            for half in range(O_BANKS):
-                nc.scalar.activation(
-                    out=x_hat[blk][:, j, half * BANK : (half + 1) * BANK],
-                    in_=o_banks[r][half][:].rearrange("p h d -> p (h d)"),
-                    func=ACT.Identity,
-                    scale=rstd[:, 0:1],
-                    bias=shift[:, 0:1],
-                )
+            nc.scalar.activation(
+                out=x_hat[blk][:, j, half * BANK : (half + 1) * BANK],
+                in_=o_banks[r][half][:].rearrange("p h d -> p (h d)"),
+                func=ACT.Identity,
+                scale=rstd[:, 0:1],
+                bias=shift[:, 0:1],
+            )
 
         y_t = {}
 
-        def flip_piece(u):
-            pair, part = divmod(u, 2)
+        def flip_piece(u, step):
+            pair, t = divmod(2 * u + step, PACK)
             blk, g = divmod(pair, PASSES)
-            if part == 0:
+            c = g * PACK + t
+            if t == 0:
                 scaled = block_pool.tile([P, PACK, ROW_TILES, P], F32)
                 y_t[pair] = scaled
-            for t in (2 * part, 2 * part + 1):
-                c = g * PACK + t
-                xt_ps = ps_short.tile([P, ROW_TILES, P], F32, tag="short")
-                for j in range(ROW_TILES):
-                    nc.tensor.transpose(
-                        xt_ps[:, j, :], x_hat[blk][:, j, c * P : (c + 1) * P], ident_f32[:]
-                    )
-                nc.scalar.activation(
-                    out=y_t[pair][:, t, :, :],
-                    in_=xt_ps[:],
-                    func=ACT.Identity,
-                    scale=gamma_beta[:, c : c + 1],
-                    bias=gamma_beta[:, CHUNKS + c : CHUNKS + c + 1],
-                )
+            xt_ps = ps_short.tile([P, ROW_TILES, P], F32, tag="short")
+            for j in range(ROW_TILES):
+                nc.tensor.transpose(xt_ps[:, j, :], x_hat[blk][:, j, c * P : (c + 1) * P], ident_f32[:])
+            nc.scalar.activation(
+                out=y_t[pair][:, t, :, :],
+                in_=xt_ps[:],
+                func=ACT.Identity,
+                scale=gamma_beta[:, c : c + 1],
+                bias=gamma_beta[:, CHUNKS + c : CHUNKS + c + 1],
+            )
 
         h_mx = {}
 
@@ -295,53 +294,60 @@ def tile_linearattention_pb_kernel(
             )
             h_mx[(pair, part)] = (h_codes, h_scales)
 
-        def project_piece(r):
+        results = {}
+
+        def project_piece(r, bank):
             blk, j = divmod(r, ROW_TILES)
             b, s = divmod(blk, BLOCKS_PER_SEQ)
             part, jj = divmod(j, QUANT_TILES)
             rows = slice(jj * P, (jj + 1) * P)
-            result = out_pool.tile([P, D_OUT], F32)
-            for bank in range(OUT_BANKS):
-                cols = slice(bank * BANK, (bank + 1) * BANK)
-                acc = ps_acc.tile([P, BANK], F32)
-                for g in range(PASSES):
-                    h_codes, h_scales = h_mx[(blk * PASSES + g, part)]
-                    nc.tensor.matmul_mx(
-                        out=acc[:],
-                        lhsT=h_codes[:, rows].bitcast(FP8X4),
-                        lhsT_scale=h_scales[:, rows],
-                        rhs=w_codes[:, g, cols].bitcast(FP8X4),
-                        rhs_scale=w_scales[:, g, cols],
-                        start=(g == 0),
-                        stop=(g == PASSES - 1),
-                    )
-                nc.vector.tensor_tensor(
-                    out=result[:, cols], in0=acc[:], in1=bias_bf[:, cols], op=ALU.add
+            cols = slice(bank * BANK, (bank + 1) * BANK)
+            if bank == 0:
+                result = out_pool.tile([P, D_OUT], F32)
+                results[r] = result
+            acc = ps_acc.tile([P, BANK], F32)
+            for g in range(PASSES):
+                h_codes, h_scales = h_mx[(blk * PASSES + g, part)]
+                nc.tensor.matmul_mx(
+                    out=acc[:],
+                    lhsT=h_codes[:, rows].bitcast(FP8X4),
+                    lhsT_scale=h_scales[:, rows],
+                    rhs=w_codes[:, g, cols].bitcast(FP8X4),
+                    rhs_scale=w_scales[:, g, cols],
+                    start=(g == 0),
+                    stop=(g == PASSES - 1),
                 )
-            out_rows = out[b, s * BLOCK : (s + 1) * BLOCK, :].rearrange(
-                "(p j) d -> p j d", j=ROW_TILES
+            nc.vector.tensor_tensor(
+                out=results[r][:, cols], in0=acc[:], in1=bias_bf[:, cols], op=ALU.add
             )
-            nc.sync.dma_start(out=out_rows[:, j, :], in_=result[:])
+            if bank == OUT_BANKS - 1:
+                out_rows = out[b, s * BLOCK : (s + 1) * BLOCK, :].rearrange(
+                    "(p j) d -> p j d", j=ROW_TILES
+                )
+                nc.sync.dma_start(out=out_rows[:, j, :], in_=results[r][:])
+
+        def run(piece, index, count, *step):
+            if 0 <= index < count:
+                piece(index, *step)
 
         for tick in range(-GATE_LEAD, ROWS + PROJECT_LAG):
-            if due(tick - NORM_LAG, ROWS):
-                norm_piece(tick - NORM_LAG)
-            if due(tick - FLIP_LAG, ROWS):
-                flip_piece(tick - FLIP_LAG)
-            if due(tick + Q_LEAD, ROWS):
-                q_piece(tick + Q_LEAD, 0)
-            if due(tick, ROWS):
-                heads_piece(tick)
-            if due(tick + Q_LEAD, ROWS):
-                q_piece(tick + Q_LEAD, 1)
-                blk, j = divmod(tick + Q_LEAD, ROW_TILES)
-                if j == ROW_TILES - 1 and blk + 2 < BLOCKS:
-                    load_q(blk + 2)
-            if due(tick + GATE_LEAD, ROWS):
-                gate_piece(tick + GATE_LEAD)
-            if due(tick - GROUP_LAG, ROWS):
-                group_piece(tick - GROUP_LAG)
-            if due(tick - W_TICK, PASSES * OUT_BANKS):
-                weight_piece(tick - W_TICK)
-            if due(tick - PROJECT_LAG, ROWS):
-                project_piece(tick - PROJECT_LAG)
+            run(group_piece, tick - GROUP_LAG, ROWS)
+            run(weight_piece, tick - W_TICK, PASSES * OUT_BANKS)
+            run(flip_piece, tick - FLIP_LAG, ROWS, 0)
+            run(heads_piece, tick, ROWS, 0)
+            run(norm_piece, tick - NORM_LAG, ROWS, 0)
+            run(flip_piece, tick - FLIP_LAG, ROWS, 1)
+            run(heads_piece, tick, ROWS, 1)
+            run(norm_piece, tick - NORM_LAG, ROWS, 1)
+            run(q_piece, tick + Q_LEAD, ROWS, 0)
+            run(heads_piece, tick, ROWS, 2)
+            run(q_piece, tick + Q_LEAD, ROWS, 1)
+            run(heads_piece, tick, ROWS, 3)
+            run(stats_piece, tick, ROWS)
+            run(gate_piece, tick + GATE_LEAD, ROWS, 0)
+            run(project_piece, tick - PROJECT_LAG, ROWS, 0)
+            run(gate_piece, tick + GATE_LEAD, ROWS, 1)
+            run(project_piece, tick - PROJECT_LAG, ROWS, 1)
+            blk, j = divmod(tick + Q_LEAD, ROW_TILES)
+            if j == ROW_TILES - 1 and 0 <= blk < BLOCKS - 2:
+                load_q(blk + 2)

@@ -22,25 +22,25 @@ K_PASS = P * PACK
 PASSES = INNER // K_PASS
 CHUNKS = INNER // P
 BANK = 512
-ROW_TILES = 4
-BLOCK = ROW_TILES * P
-BLOCKS_PER_SEQ = SEQ // BLOCK
-BLOCKS = BATCH * BLOCKS_PER_SEQ
+ROW_TILES = 2
+GROUP = ROW_TILES * P
+GROUPS_PER_SEQ = SEQ // GROUP
+GROUPS = BATCH * GROUPS_PER_SEQ
+ROWS = GROUPS * ROW_TILES
+PAIRS = GROUPS * PASSES
 HEADS_PER_BANK = BANK // HEAD_DIM
 O_BANKS = INNER // BANK
 OUT_BANKS = D_OUT // BANK
-ROWS = BLOCKS * ROW_TILES
-ALL_PASSES = BLOCKS * PASSES
-QUANT_TILES = 2
-QUANTS = ROW_TILES // QUANT_TILES
+CHUNKS_PER_BANK = BANK // GROUP
 
 GATE_LEAD = 3
 Q_LEAD = 1
-NORM_LAG = 1
-FLIP_LAG = ROW_TILES + NORM_LAG
-GROUP_LAG = FLIP_LAG + 2
-PROJECT_LAG = GROUP_LAG + PASSES * QUANTS - 1
-W_TICK = 4
+STATS_LAG = 1
+FLIP_LAG = ROW_TILES + STATS_LAG + 1
+PRODUCT_LAG = FLIP_LAG + 1
+PROJECT_LAG = PRODUCT_LAG + PASSES
+W_TICK = 2
+Q_BUFS = 4
 
 FLOPS = 2 * BATCH * SEQ * (HEADS * 2 * HEAD_DIM * HEAD_DIM + HEAD_DIM * INNER + INNER * D_OUT)
 
@@ -51,15 +51,16 @@ def tile_linearattention_pb_kernel(
     nc = tc.nc
     with ExitStack() as ctx:
         const = ctx.enter_context(tc.tile_pool(name="const", bufs=1))
-        q_pool = ctx.enter_context(tc.tile_pool(name="q", bufs=2 * O_BANKS))
+        q_pool = ctx.enter_context(tc.tile_pool(name="q", bufs=Q_BUFS))
         qt_pool = ctx.enter_context(tc.tile_pool(name="qt", bufs=3))
-        block_pool = ctx.enter_context(tc.tile_pool(name="block", bufs=2))
-        gate_pool = ctx.enter_context(tc.tile_pool(name="gate", bufs=6))
-        mx_pool = ctx.enter_context(tc.tile_pool(name="mx", bufs=2 * PASSES * QUANTS))
+        x_pool = ctx.enter_context(tc.tile_pool(name="x", bufs=4))
+        y_pool = ctx.enter_context(tc.tile_pool(name="y", bufs=3))
+        gate_pool = ctx.enter_context(tc.tile_pool(name="gate", bufs=GATE_LEAD + PRODUCT_LAG + 2))
+        mx_pool = ctx.enter_context(tc.tile_pool(name="mx", bufs=6))
         stat_pool = ctx.enter_context(tc.tile_pool(name="stat", bufs=4))
         out_pool = ctx.enter_context(tc.tile_pool(name="outs", bufs=4))
-        ps_short = ctx.enter_context(tc.psum_pool(name="ps_short", bufs=3))
-        ps_o = ctx.enter_context(tc.psum_pool(name="ps_o", bufs=3))
+        ps_ring = ctx.enter_context(tc.psum_pool(name="ps_ring", bufs=4))
+        ps_o = ctx.enter_context(tc.psum_pool(name="ps_o", bufs=2))
         ps_acc = ctx.enter_context(tc.psum_pool(name="ps_acc", bufs=2))
         ctx.enter_context(tc.manual_schedule())
 
@@ -70,7 +71,7 @@ def tile_linearattention_pb_kernel(
         neg_half = const.tile([P, 1], F32)
         nc.vector.memset(neg_half[:], -0.5)
 
-        g_sb = const.tile([P, BLOCKS, ROW_TILES, HEAD_DIM], BF16)
+        g_sb = const.tile([P, GROUPS, ROW_TILES, HEAD_DIM], BF16)
         nc.sync.dma_start(
             out=g_sb[:].rearrange("p s j g -> p s (j g)"),
             in_=g_low.rearrange("b (s p j) g -> p (b s) (j g)", p=P, j=ROW_TILES),
@@ -96,37 +97,44 @@ def tile_linearattention_pb_kernel(
 
         q_tiles = {}
 
-        def load_q(blk):
-            b, s = divmod(blk, BLOCKS_PER_SEQ)
-            rows = slice(s * BLOCK, (s + 1) * BLOCK)
-            for half in range(O_BANKS):
-                heads = slice(half * HEADS_PER_BANK, (half + 1) * HEADS_PER_BANK)
-                q_sb = q_pool.tile([P, HEADS_PER_BANK, ROW_TILES, 2 * HEAD_DIM], BF16)
-                nc.sync.dma_start(
-                    out=q_sb[:].rearrange("p h j k -> p h (j k)"),
-                    in_=q_rot[b, heads, rows, :].rearrange("h (p j) k -> p h (j k)", j=ROW_TILES),
-                )
-                q_tiles[(blk, half)] = q_sb
+        def load_q(grp):
+            b, s = divmod(grp, GROUPS_PER_SEQ)
+            q_sb = q_pool.tile([P, HEADS, ROW_TILES, 2 * HEAD_DIM], BF16)
+            nc.sync.dma_start(
+                out=q_sb[:].rearrange("p h j k -> p h (j k)"),
+                in_=q_rot[b, :, s * GROUP : (s + 1) * GROUP, :].rearrange(
+                    "h (p j) k -> p h (j k)", j=ROW_TILES
+                ),
+            )
+            q_tiles[grp] = q_sb
+
+        w_sb = const.tile([P, CHUNKS, D_OUT], BF16)
+        w_view = w_out.rearrange("(c p) n -> p c n", p=P)
+
+        def load_w(g):
+            chunks = slice(g * PACK, (g + 1) * PACK)
+            nc.sync.dma_start(out=w_sb[:, chunks, :], in_=w_view[:, chunks, :])
 
         load_q(0)
         load_kv(0)
         load_q(1)
-        w_sb = const.tile([P, CHUNKS, D_OUT], BF16)
-        w_view = w_out.rearrange("(c p) n -> p c n", p=P)
-        for g in range(PASSES):
-            chunks = slice(g * PACK, (g + 1) * PACK)
-            nc.sync.dma_start(out=w_sb[:, chunks, :], in_=w_view[:, chunks, :])
+        load_w(0)
+        load_q(2)
+        load_w(1)
+        load_q(3)
         load_kv(1)
         bias_bf = const.tile([P, D_OUT], BF16)
         nc.sync.dma_start(out=bias_bf[:], in_=b_out.partition_broadcast(P))
 
-        g_t = const.tile([P, BLOCKS, ROW_TILES, P], BF16)
-        for blk in range(BLOCKS):
-            gt_ps = ps_short.tile([P, ROW_TILES, P], BF16, tag="short")
-            for j in range(ROW_TILES):
-                nc.tensor.transpose(gt_ps[:, j, :], g_sb[:, blk, j, :], ident_bf[:])
-            nc.vector.tensor_copy(out=g_t[:, blk, :, :], in_=gt_ps[:])
-        gb_ps = ps_short.tile([P, P], BF16, tag="short")
+        g_t = const.tile([P, GROUPS, ROW_TILES, P], BF16)
+        groups_per_bank = 2 * BANK // GROUP
+        for first in range(0, GROUPS, groups_per_bank):
+            gt_ps = ps_ring.tile([P, groups_per_bank, ROW_TILES, P], BF16, tag="ring")
+            for i in range(groups_per_bank):
+                for j in range(ROW_TILES):
+                    nc.tensor.transpose(gt_ps[:, i, j, :], g_sb[:, first + i, j, :], ident_bf[:])
+            nc.vector.tensor_copy(out=g_t[:, first : first + groups_per_bank, :, :], in_=gt_ps[:])
+        gb_ps = ps_ring.tile([P, P], BF16, tag="ring")
         nc.tensor.transpose(gb_ps[:], gb_rows[:], ident_bf[:])
         gamma_beta = const.tile([P, 2 * CHUNKS], F32)
         nc.vector.tensor_copy(out=gamma_beta[:], in_=gb_ps[:, 0 : 2 * CHUNKS])
@@ -154,19 +162,18 @@ def tile_linearattention_pb_kernel(
 
         gates = {}
 
-        def gate_piece(v, step):
-            pair, j = divmod(2 * v + step, ROW_TILES)
-            blk, g = divmod(pair, PASSES)
+        def gate_piece(pair, j):
+            grp, g = divmod(pair, PASSES)
             if j == 0:
                 gate = gate_pool.tile([P, ROW_TILES, P, PACK], F32)
                 gates[pair] = gate
-            u_ps = ps_short.tile([P, PACK, P], F32, tag="short")
+            u_ps = ps_ring.tile([P, PACK, P], F32, tag="ring")
             for t in range(PACK):
                 c = g * PACK + t
                 nc.tensor.matmul(
                     out=u_ps[:, t, :],
                     lhsT=wg_sb[:, c * P : (c + 1) * P],
-                    rhs=g_t[:, blk, j, :],
+                    rhs=g_t[:, grp, j, :],
                     start=True,
                     stop=True,
                 )
@@ -177,52 +184,58 @@ def tile_linearattention_pb_kernel(
         q_t = {}
 
         def q_piece(r, half):
-            blk, j = divmod(r, ROW_TILES)
+            grp, j = divmod(r, ROW_TILES)
             if half == 0:
                 words = qt_pool.tile([P, HEADS, P], F32)
                 q_t[r] = words
-            tq_ps = ps_short.tile([P, HEADS_PER_BANK, P], F32, tag="short")
+            tq_ps = ps_ring.tile([P, HEADS_PER_BANK, P], F32, tag="ring")
             for hh in range(HEADS_PER_BANK):
-                nc.tensor.transpose(
-                    tq_ps[:, hh, :], q_tiles[(blk, half)][:, hh, j, :].bitcast(F32), ident_f32[:]
-                )
+                h = half * HEADS_PER_BANK + hh
+                nc.tensor.transpose(tq_ps[:, hh, :], q_tiles[grp][:, h, j, :].bitcast(F32), ident_f32[:])
             heads = slice(half * HEADS_PER_BANK, (half + 1) * HEADS_PER_BANK)
             nc.scalar.copy(out=q_t[r][:, heads, :], in_=tq_ps[:])
 
         o_banks = {}
-        norm_terms = {}
-
-        stats_of = {}
 
         def heads_piece(r, quarter):
-            b = r // (ROW_TILES * BLOCKS_PER_SEQ)
+            b = r // (ROW_TILES * GROUPS_PER_SEQ)
             half, second = divmod(quarter, 2)
-            if quarter == 0:
-                stats = stat_pool.tile([P, O_BANKS, 6], F32)
-                stats_of[r] = stats
-                o_banks[r] = []
             if second == 0:
                 o_ps = ps_o.tile([P, HEADS_PER_BANK, HEAD_DIM], F32)
-                o_banks[r].append(o_ps)
+                o_banks[(r, half)] = o_ps
             for hh in (2 * second, 2 * second + 1):
                 h = half * HEADS_PER_BANK + hh
                 pairs = q_t[r][:, h, :].bitcast(BF16).rearrange("w (n e) -> w n e", e=2)
                 for e in range(2):
                     nc.tensor.matmul(
-                        out=o_banks[r][half][:, hh, :],
+                        out=o_banks[(r, half)][:, hh, :],
                         lhsT=pairs[:, :, e],
                         rhs=kv_sb[:, b * HEADS + h, e, :],
                         start=(e == 0),
                         stop=(e == 1),
                     )
-            if second == 1:
-                nc.vector.bn_stats(
-                    out=stats_of[r][:, half, :], in_=o_banks[r][half][:].rearrange("p h d -> p (h d)")
-                )
 
-        def stats_piece(r):
+        x_rows = {}
+
+        def drain_piece(r, half):
+            grp, j = divmod(r, ROW_TILES)
+            if j == 0 and half == 0:
+                o_rows = x_pool.tile([P, ROW_TILES, INNER], F32)
+                x_rows[grp] = o_rows
+            nc.scalar.copy(
+                out=x_rows[grp][:, j, half * BANK : (half + 1) * BANK],
+                in_=o_banks[(r, half)][:].rearrange("p h d -> p (h d)"),
+            )
+
+        def norm_piece(r):
+            grp, j = divmod(r, ROW_TILES)
+            stats = stat_pool.tile([P, O_BANKS, 6], F32)
+            for half in range(O_BANKS):
+                nc.vector.bn_stats(
+                    out=stats[:, half, :], in_=x_rows[grp][:, j, half * BANK : (half + 1) * BANK]
+                )
             mean_var = stat_pool.tile([P, 2], F32)
-            nc.vector.bn_aggr(out=mean_var[:], in_=stats_of[r][:].rearrange("p a s -> p (a s)"))
+            nc.vector.bn_aggr(out=mean_var[:], in_=stats[:].rearrange("p a s -> p (a s)"))
             var_eps = stat_pool.tile([P, 1], F32)
             nc.vector.tensor_scalar(
                 out=var_eps[:], in0=mean_var[:, 1:2], scalar1=LN_EPS, scalar2=None, op0=ALU.add
@@ -235,79 +248,74 @@ def tile_linearattention_pb_kernel(
             nc.gpsimd.tensor_tensor(out=rstd[:], in0=var_eps[:], in1=neg_half[:], op=ALU.pow)
             shift = stat_pool.tile([P, 1], F32)
             nc.gpsimd.tensor_tensor(out=shift[:], in0=neg_mean[:], in1=rstd[:], op=ALU.mult)
-            norm_terms[r] = (rstd, shift)
-
-        x_hat = {}
-
-        def norm_piece(r, half):
-            blk, j = divmod(r, ROW_TILES)
-            if j == 0 and half == 0:
-                normed = block_pool.tile([P, ROW_TILES, INNER], F32)
-                x_hat[blk] = normed
-            rstd, shift = norm_terms[r]
-            nc.scalar.activation(
-                out=x_hat[blk][:, j, half * BANK : (half + 1) * BANK],
-                in_=o_banks[r][half][:].rearrange("p h d -> p (h d)"),
-                func=ACT.Identity,
-                scale=rstd[:, 0:1],
-                bias=shift[:, 0:1],
-            )
+            for half in range(O_BANKS):
+                cols = slice(half * BANK, (half + 1) * BANK)
+                nc.gpsimd.tensor_scalar(
+                    out=x_rows[grp][:, j, cols],
+                    in0=x_rows[grp][:, j, cols],
+                    scalar1=rstd[:, 0:1],
+                    scalar2=shift[:, 0:1],
+                    op0=ALU.mult,
+                    op1=ALU.add,
+                )
 
         y_t = {}
 
-        def flip_piece(u, step):
-            pair, t = divmod(2 * u + step, PACK)
-            blk, g = divmod(pair, PASSES)
-            c = g * PACK + t
-            if t == 0:
-                scaled = block_pool.tile([P, PACK, ROW_TILES, P], F32)
+        def flip_piece(pair, step):
+            grp, g = divmod(pair, PASSES)
+            if step == 0:
+                scaled = y_pool.tile([P, PACK, ROW_TILES, P], F32)
                 y_t[pair] = scaled
-            xt_ps = ps_short.tile([P, ROW_TILES, P], F32, tag="short")
-            for j in range(ROW_TILES):
-                nc.tensor.transpose(xt_ps[:, j, :], x_hat[blk][:, j, c * P : (c + 1) * P], ident_f32[:])
-            nc.scalar.activation(
-                out=y_t[pair][:, t, :, :],
-                in_=xt_ps[:],
-                func=ACT.Identity,
-                scale=gamma_beta[:, c : c + 1],
-                bias=gamma_beta[:, CHUNKS + c : CHUNKS + c + 1],
-            )
+            xt_ps = ps_ring.tile([P, CHUNKS_PER_BANK, ROW_TILES, P], F32, tag="ring")
+            for i in range(CHUNKS_PER_BANK):
+                c = g * PACK + step * CHUNKS_PER_BANK + i
+                for j in range(ROW_TILES):
+                    nc.tensor.transpose(
+                        xt_ps[:, i, j, :], x_rows[grp][:, j, c * P : (c + 1) * P], ident_f32[:]
+                    )
+            for i in range(CHUNKS_PER_BANK):
+                t = step * CHUNKS_PER_BANK + i
+                c = g * PACK + t
+                nc.scalar.activation(
+                    out=y_t[pair][:, t, :, :],
+                    in_=xt_ps[:, i, :, :],
+                    func=ACT.Identity,
+                    scale=gamma_beta[:, c : c + 1],
+                    bias=gamma_beta[:, CHUNKS + c : CHUNKS + c + 1],
+                )
 
         h_mx = {}
 
-        def group_piece(i):
-            pair, part = divmod(i, QUANTS)
-            tiles = slice(part * QUANT_TILES, (part + 1) * QUANT_TILES)
-            h_grouped = block_pool.tile([P, QUANT_TILES * P, PACK], BF16, align_bytes=64)
+        def product_piece(pair):
+            h_grouped = y_pool.tile([P, GROUP, PACK], BF16, align_bytes=64)
             nc.vector.tensor_tensor(
                 out=h_grouped[:],
-                in0=y_t[pair][:, :, tiles, :].rearrange("p t j n -> p (j n) t"),
-                in1=gates[pair][:, tiles, :, :].rearrange("p j n t -> p (j n) t"),
+                in0=y_t[pair][:].rearrange("p t j n -> p (j n) t"),
+                in1=gates[pair][:].rearrange("p j n t -> p (j n) t"),
                 op=ALU.mult,
             )
-            h_codes = mx_pool.tile([P, QUANT_TILES * P], U32, align_bytes=64)
-            h_scales = mx_pool.tile([P, QUANT_TILES * P], U8, align_bytes=64)
+            h_codes = mx_pool.tile([P, GROUP], U32, align_bytes=64)
+            h_scales = mx_pool.tile([P, GROUP], U8, align_bytes=64)
             nc.vector.quantize_mx(
                 out=h_codes[:].bitcast(FP8X4),
                 scales=h_scales[:],
                 in_=h_grouped[:].rearrange("p m t -> p (m t)"),
             )
-            h_mx[(pair, part)] = (h_codes, h_scales)
+            h_mx[pair] = (h_codes, h_scales)
 
         results = {}
 
         def project_piece(r, bank):
-            blk, j = divmod(r, ROW_TILES)
-            b, s = divmod(blk, BLOCKS_PER_SEQ)
-            part, jj = divmod(j, QUANT_TILES)
-            rows = slice(jj * P, (jj + 1) * P)
+            grp, j = divmod(r, ROW_TILES)
+            b, s = divmod(grp, GROUPS_PER_SEQ)
+            rows = slice(j * P, (j + 1) * P)
             cols = slice(bank * BANK, (bank + 1) * BANK)
             if bank == 0:
                 result = out_pool.tile([P, D_OUT], F32)
                 results[r] = result
             acc = ps_acc.tile([P, BANK], F32)
             for g in range(PASSES):
-                h_codes, h_scales = h_mx[(blk * PASSES + g, part)]
+                h_codes, h_scales = h_mx[grp * PASSES + g]
                 nc.tensor.matmul_mx(
                     out=acc[:],
                     lhsT=h_codes[:, rows].bitcast(FP8X4),
@@ -321,7 +329,7 @@ def tile_linearattention_pb_kernel(
                 out=results[r][:, cols], in0=acc[:], in1=bias_bf[:, cols], op=ALU.add
             )
             if bank == OUT_BANKS - 1:
-                out_rows = out[b, s * BLOCK : (s + 1) * BLOCK, :].rearrange(
+                out_rows = out[b, s * GROUP : (s + 1) * GROUP, :].rearrange(
                     "(p j) d -> p j d", j=ROW_TILES
                 )
                 nc.sync.dma_start(out=out_rows[:, j, :], in_=results[r][:])
@@ -331,23 +339,23 @@ def tile_linearattention_pb_kernel(
                 piece(index, *step)
 
         for tick in range(-GATE_LEAD, ROWS + PROJECT_LAG):
-            run(group_piece, tick - GROUP_LAG, ROWS)
+            run(product_piece, tick - PRODUCT_LAG, PAIRS)
             run(weight_piece, tick - W_TICK, PASSES * OUT_BANKS)
-            run(flip_piece, tick - FLIP_LAG, ROWS, 0)
+            run(norm_piece, tick - STATS_LAG, ROWS)
+            run(flip_piece, tick - FLIP_LAG, PAIRS, 0)
             run(heads_piece, tick, ROWS, 0)
-            run(norm_piece, tick - NORM_LAG, ROWS, 0)
-            run(flip_piece, tick - FLIP_LAG, ROWS, 1)
+            run(flip_piece, tick - FLIP_LAG, PAIRS, 1)
             run(heads_piece, tick, ROWS, 1)
-            run(norm_piece, tick - NORM_LAG, ROWS, 1)
+            run(drain_piece, tick, ROWS, 0)
             run(q_piece, tick + Q_LEAD, ROWS, 0)
             run(heads_piece, tick, ROWS, 2)
             run(q_piece, tick + Q_LEAD, ROWS, 1)
             run(heads_piece, tick, ROWS, 3)
-            run(stats_piece, tick, ROWS)
-            run(gate_piece, tick + GATE_LEAD, ROWS, 0)
+            run(drain_piece, tick, ROWS, 1)
+            run(gate_piece, tick + GATE_LEAD, PAIRS, 0)
             run(project_piece, tick - PROJECT_LAG, ROWS, 0)
-            run(gate_piece, tick + GATE_LEAD, ROWS, 1)
+            run(gate_piece, tick + GATE_LEAD, PAIRS, 1)
             run(project_piece, tick - PROJECT_LAG, ROWS, 1)
-            blk, j = divmod(tick + Q_LEAD, ROW_TILES)
-            if j == ROW_TILES - 1 and 0 <= blk < BLOCKS - 2:
-                load_q(blk + 2)
+            grp, j = divmod(tick + Q_LEAD, ROW_TILES)
+            if j == ROW_TILES - 1 and 0 <= grp < GROUPS - Q_BUFS:
+                load_q(grp + Q_BUFS)

@@ -193,22 +193,23 @@ def tile_linearattention_pb_kernel(
                 h = half * HEADS_PER_BANK + hh
                 nc.tensor.transpose(tq_ps[:, hh, :], q_tiles[grp][:, h, j, :].bitcast(F32), ident_f32[:])
             heads = slice(half * HEADS_PER_BANK, (half + 1) * HEADS_PER_BANK)
-            nc.scalar.copy(out=q_t[r][:, heads, :], in_=tq_ps[:])
+            if half == 0:
+                nc.vector.tensor_copy(out=q_t[r][:, heads, :], in_=tq_ps[:])
+            else:
+                nc.scalar.copy(out=q_t[r][:, heads, :], in_=tq_ps[:])
 
         o_banks = {}
 
-        def heads_piece(r, quarter):
+        def heads_piece(r, half):
             b = r // (ROW_TILES * GROUPS_PER_SEQ)
-            half, second = divmod(quarter, 2)
-            if second == 0:
-                o_ps = ps_o.tile([P, HEADS_PER_BANK, HEAD_DIM], F32)
-                o_banks[(r, half)] = o_ps
-            for hh in (2 * second, 2 * second + 1):
+            o_ps = ps_o.tile([P, HEADS_PER_BANK, HEAD_DIM], F32)
+            o_banks[(r, half)] = o_ps
+            for hh in range(HEADS_PER_BANK):
                 h = half * HEADS_PER_BANK + hh
                 pairs = q_t[r][:, h, :].bitcast(BF16).rearrange("w (n e) -> w n e", e=2)
                 for e in range(2):
                     nc.tensor.matmul(
-                        out=o_banks[(r, half)][:, hh, :],
+                        out=o_ps[:, hh, :],
                         lhsT=pairs[:, :, e],
                         rhs=kv_sb[:, b * HEADS + h, e, :],
                         start=(e == 0),
@@ -227,27 +228,31 @@ def tile_linearattention_pb_kernel(
                 in_=o_banks[(r, half)][:].rearrange("p h d -> p (h d)"),
             )
 
-        def norm_piece(r):
+        stats_of = {}
+
+        def stats_piece(r):
             grp, j = divmod(r, ROW_TILES)
             stats = stat_pool.tile([P, O_BANKS, 6], F32)
             for half in range(O_BANKS):
                 nc.vector.bn_stats(
                     out=stats[:, half, :], in_=x_rows[grp][:, j, half * BANK : (half + 1) * BANK]
                 )
+            stats_of[r] = stats
+
+        def norm_piece(r):
+            grp, j = divmod(r, ROW_TILES)
             mean_var = stat_pool.tile([P, 2], F32)
-            nc.vector.bn_aggr(out=mean_var[:], in_=stats[:].rearrange("p a s -> p (a s)"))
+            nc.vector.bn_aggr(out=mean_var[:], in_=stats_of[r][:].rearrange("p a s -> p (a s)"))
             var_eps = stat_pool.tile([P, 1], F32)
-            nc.vector.tensor_scalar(
-                out=var_eps[:], in0=mean_var[:, 1:2], scalar1=LN_EPS, scalar2=None, op0=ALU.add
-            )
-            neg_mean = stat_pool.tile([P, 1], F32)
-            nc.vector.tensor_scalar(
-                out=neg_mean[:], in0=mean_var[:, 0:1], scalar1=-1.0, scalar2=None, op0=ALU.mult
+            nc.gpsimd.tensor_scalar(
+                out=var_eps[:], in0=mean_var[:, 1:2], scalar1=1.0, scalar2=LN_EPS, op0=ALU.mult, op1=ALU.add
             )
             rstd = stat_pool.tile([P, 1], F32)
             nc.gpsimd.tensor_tensor(out=rstd[:], in0=var_eps[:], in1=neg_half[:], op=ALU.pow)
             shift = stat_pool.tile([P, 1], F32)
-            nc.gpsimd.tensor_tensor(out=shift[:], in0=neg_mean[:], in1=rstd[:], op=ALU.mult)
+            nc.gpsimd.tensor_scalar(
+                out=shift[:], in0=mean_var[:, 0:1], scalar1=rstd[:, 0:1], scalar2=-1.0, op0=ALU.mult, op1=ALU.mult
+            )
             for half in range(O_BANKS):
                 cols = slice(half * BANK, (half + 1) * BANK)
                 nc.gpsimd.tensor_scalar(
@@ -284,6 +289,7 @@ def tile_linearattention_pb_kernel(
                     bias=gamma_beta[:, CHUNKS + c : CHUNKS + c + 1],
                 )
 
+        h_bf = {}
         h_mx = {}
 
         def product_piece(pair):
@@ -294,12 +300,15 @@ def tile_linearattention_pb_kernel(
                 in1=gates[pair][:].rearrange("p j n t -> p (j n) t"),
                 op=ALU.mult,
             )
+            h_bf[pair] = h_grouped
+
+        def quantise_piece(pair):
             h_codes = mx_pool.tile([P, GROUP], U32, align_bytes=64)
             h_scales = mx_pool.tile([P, GROUP], U8, align_bytes=64)
             nc.vector.quantize_mx(
                 out=h_codes[:].bitcast(FP8X4),
                 scales=h_scales[:],
-                in_=h_grouped[:].rearrange("p m t -> p (m t)"),
+                in_=h_bf[pair][:].rearrange("p m t -> p (m t)"),
             )
             h_mx[pair] = (h_codes, h_scales)
 
@@ -340,17 +349,17 @@ def tile_linearattention_pb_kernel(
 
         for tick in range(-GATE_LEAD, ROWS + PROJECT_LAG):
             run(product_piece, tick - PRODUCT_LAG, PAIRS)
-            run(weight_piece, tick - W_TICK, PASSES * OUT_BANKS)
+            run(stats_piece, tick - STATS_LAG, ROWS)
+            run(quantise_piece, tick - PRODUCT_LAG, PAIRS)
             run(norm_piece, tick - STATS_LAG, ROWS)
+            run(weight_piece, tick - W_TICK, PASSES * OUT_BANKS)
             run(flip_piece, tick - FLIP_LAG, PAIRS, 0)
-            run(heads_piece, tick, ROWS, 0)
             run(flip_piece, tick - FLIP_LAG, PAIRS, 1)
-            run(heads_piece, tick, ROWS, 1)
+            run(heads_piece, tick, ROWS, 0)
             run(drain_piece, tick, ROWS, 0)
             run(q_piece, tick + Q_LEAD, ROWS, 0)
-            run(heads_piece, tick, ROWS, 2)
             run(q_piece, tick + Q_LEAD, ROWS, 1)
-            run(heads_piece, tick, ROWS, 3)
+            run(heads_piece, tick, ROWS, 1)
             run(drain_piece, tick, ROWS, 1)
             run(gate_piece, tick + GATE_LEAD, PAIRS, 0)
             run(project_piece, tick - PROJECT_LAG, ROWS, 0)

@@ -193,10 +193,7 @@ def tile_linearattention_pb_kernel(
                 h = half * HEADS_PER_BANK + hh
                 nc.tensor.transpose(tq_ps[:, hh, :], q_tiles[grp][:, h, j, :].bitcast(F32), ident_f32[:])
             heads = slice(half * HEADS_PER_BANK, (half + 1) * HEADS_PER_BANK)
-            if half == 0:
-                nc.vector.tensor_copy(out=q_t[r][:, heads, :], in_=tq_ps[:])
-            else:
-                nc.scalar.copy(out=q_t[r][:, heads, :], in_=tq_ps[:])
+            nc.scalar.copy(out=q_t[r][:, heads, :], in_=tq_ps[:])
 
         o_banks = {}
 
@@ -244,25 +241,23 @@ def tile_linearattention_pb_kernel(
             mean_var = stat_pool.tile([P, 2], F32)
             nc.vector.bn_aggr(out=mean_var[:], in_=stats_of[r][:].rearrange("p a s -> p (a s)"))
             var_eps = stat_pool.tile([P, 1], F32)
-            nc.gpsimd.tensor_scalar(
-                out=var_eps[:], in0=mean_var[:, 1:2], scalar1=1.0, scalar2=LN_EPS, op0=ALU.mult, op1=ALU.add
+            nc.vector.tensor_scalar(
+                out=var_eps[:], in0=mean_var[:, 1:2], scalar1=LN_EPS, scalar2=None, op0=ALU.add
+            )
+            neg_mean = stat_pool.tile([P, 1], F32)
+            nc.vector.tensor_scalar(
+                out=neg_mean[:], in0=mean_var[:, 0:1], scalar1=-1.0, scalar2=None, op0=ALU.mult
             )
             rstd = stat_pool.tile([P, 1], F32)
             nc.gpsimd.tensor_tensor(out=rstd[:], in0=var_eps[:], in1=neg_half[:], op=ALU.pow)
-            shift = stat_pool.tile([P, 1], F32)
             nc.gpsimd.tensor_scalar(
-                out=shift[:], in0=mean_var[:, 0:1], scalar1=rstd[:, 0:1], scalar2=-1.0, op0=ALU.mult, op1=ALU.mult
+                out=x_rows[grp][:, j, :],
+                in0=x_rows[grp][:, j, :],
+                scalar1=neg_mean[:, 0:1],
+                scalar2=rstd[:, 0:1],
+                op0=ALU.add,
+                op1=ALU.mult,
             )
-            for half in range(O_BANKS):
-                cols = slice(half * BANK, (half + 1) * BANK)
-                nc.gpsimd.tensor_scalar(
-                    out=x_rows[grp][:, j, cols],
-                    in0=x_rows[grp][:, j, cols],
-                    scalar1=rstd[:, 0:1],
-                    scalar2=shift[:, 0:1],
-                    op0=ALU.mult,
-                    op1=ALU.add,
-                )
 
         y_t = {}
 

from contextlib import ExitStack

import concourse.mybir as mybir
from concourse.masks import make_identity

F32 = mybir.dt.float32
BF16 = mybir.dt.bfloat16
U32 = mybir.dt.uint32
U8 = mybir.dt.uint8
FP8X4 = mybir.dt.float8_e4m3fn_x4
ACT = mybir.ActivationFunctionType
ALU = mybir.AluOpType

P = 128
BATCH, SEQ, HEADS, HEAD_DIM = 2, 1024, 8, 128
INNER = HEADS * HEAD_DIM
D_OUT = 1024
LN_EPS = 1e-5

PACK = 4
K_PASS = P * PACK
PASSES = INNER // K_PASS
CHUNKS = INNER // P
BANK = 512
ROW_TILES = 2
GROUP = ROW_TILES * P
GROUPS_PER_SEQ = SEQ // GROUP
GROUPS = BATCH * GROUPS_PER_SEQ
ROWS = GROUPS * ROW_TILES
PAIRS = GROUPS * PASSES
HEADS_PER_BANK = BANK // HEAD_DIM
O_BANKS = INNER // BANK
OUT_BANKS = D_OUT // BANK
CHUNKS_PER_BANK = BANK // GROUP

GATE_LEAD = 3
Q_LEAD = 1
STATS_LAG = 1
FLIP_LAG = ROW_TILES + STATS_LAG + 1
PRODUCT_LAG = FLIP_LAG + 1
PROJECT_LAG = PRODUCT_LAG + PASSES
W_TICK = 2
Q_BUFS = 4

FLOPS = 2 * BATCH * SEQ * (HEADS * 2 * HEAD_DIM * HEAD_DIM + HEAD_DIM * INNER + INNER * D_OUT)


def tile_linearattention_pb_kernel(
    tc, q_rot, kv, g_low, w_g2, ln_gamma, ln_beta, w_out, b_out, out
):
    nc = tc.nc
    with ExitStack() as ctx:
        const = ctx.enter_context(tc.tile_pool(name="const", bufs=1))
        q_pool = ctx.enter_context(tc.tile_pool(name="q", bufs=Q_BUFS))
        qt_pool = ctx.enter_context(tc.tile_pool(name="qt", bufs=3))
        x_pool = ctx.enter_context(tc.tile_pool(name="x", bufs=4))
        y_pool = ctx.enter_context(tc.tile_pool(name="y", bufs=3))
        gate_pool = ctx.enter_context(tc.tile_pool(name="gate", bufs=GATE_LEAD + PRODUCT_LAG + 2))
        mx_pool = ctx.enter_context(tc.tile_pool(name="mx", bufs=6))
        stat_pool = ctx.enter_context(tc.tile_pool(name="stat", bufs=4))
        out_pool = ctx.enter_context(tc.tile_pool(name="outs", bufs=4))
        ps_ring = ctx.enter_context(tc.psum_pool(name="ps_ring", bufs=4))
        ps_o = ctx.enter_context(tc.psum_pool(name="ps_o", bufs=2))
        ps_acc = ctx.enter_context(tc.psum_pool(name="ps_acc", bufs=2))
        ctx.enter_context(tc.manual_schedule())

        ident_bf = const.tile([P, P], BF16)
        make_identity(nc, ident_bf[:])
        ident_f32 = const.tile([P, P], F32)
        make_identity(nc, ident_f32[:])
        neg_half = const.tile([P, 1], F32)
        nc.vector.memset(neg_half[:], -0.5)

        g_sb = const.tile([P, GROUPS, ROW_TILES, HEAD_DIM], BF16)
        nc.sync.dma_start(
            out=g_sb[:].rearrange("p s j g -> p s (j g)"),
            in_=g_low.rearrange("b (s p j) g -> p (b s) (j g)", p=P, j=ROW_TILES),
        )
        wg_sb = const.tile([P, INNER], BF16)
        nc.sync.dma_start(out=wg_sb[:], in_=w_g2)

        gb_rows = const.tile([P, P], BF16)
        nc.vector.memset(gb_rows[:], 0.0)
        nc.sync.dma_start(out=gb_rows[0:CHUNKS, :], in_=ln_gamma.rearrange("(c p) -> c p", p=P))
        nc.sync.dma_start(
            out=gb_rows[CHUNKS : 2 * CHUNKS, :], in_=ln_beta.rearrange("(c p) -> c p", p=P)
        )

        kv_sb = const.tile([P, BATCH * HEADS, 2, HEAD_DIM], BF16)
        kv_view = kv.rearrange("b h (w e) d -> w (b h) (e d)", e=2)

        def load_kv(b):
            heads = slice(b * HEADS, (b + 1) * HEADS)
            nc.sync.dma_start(
                out=kv_sb[:, heads, :, :].rearrange("w h e d -> w h (e d)"), in_=kv_view[:, heads, :]
            )

        q_tiles = {}

        def load_q(grp):
            b, s = divmod(grp, GROUPS_PER_SEQ)
            q_sb = q_pool.tile([P, HEADS, ROW_TILES, 2 * HEAD_DIM], BF16)
            nc.sync.dma_start(
                out=q_sb[:].rearrange("p h j k -> p h (j k)"),
                in_=q_rot[b, :, s * GROUP : (s + 1) * GROUP, :].rearrange(
                    "h (p j) k -> p h (j k)", j=ROW_TILES
                ),
            )
            q_tiles[grp] = q_sb

        w_sb = const.tile([P, CHUNKS, D_OUT], BF16)
        w_view = w_out.rearrange("(c p) n -> p c n", p=P)

        def load_w(g):
            chunks = slice(g * PACK, (g + 1) * PACK)
            nc.sync.dma_start(out=w_sb[:, chunks, :], in_=w_view[:, chunks, :])

        load_q(0)
        load_kv(0)
        load_q(1)
        load_w(0)
        load_q(2)
        load_w(1)
        load_q(3)
        load_kv(1)
        bias_bf = const.tile([P, D_OUT], BF16)
        nc.sync.dma_start(out=bias_bf[:], in_=b_out.partition_broadcast(P))

        g_t = const.tile([P, GROUPS, ROW_TILES, P], BF16)
        groups_per_bank = 2 * BANK // GROUP
        for first in range(0, GROUPS, groups_per_bank):
            gt_ps = ps_ring.tile([P, groups_per_bank, ROW_TILES, P], BF16, tag="ring")
            for i in range(groups_per_bank):
                for j in range(ROW_TILES):
                    nc.tensor.transpose(gt_ps[:, i, j, :], g_sb[:, first + i, j, :], ident_bf[:])
            nc.vector.tensor_copy(out=g_t[:, first : first + groups_per_bank, :, :], in_=gt_ps[:])
        gb_ps = ps_ring.tile([P, P], BF16, tag="ring")
        nc.tensor.transpose(gb_ps[:], gb_rows[:], ident_bf[:])
        gamma_beta = const.tile([P, 2 * CHUNKS], F32)
        nc.vector.tensor_copy(out=gamma_beta[:], in_=gb_ps[:, 0 : 2 * CHUNKS])

        w_codes = const.tile([P, PASSES, D_OUT], U32, align_bytes=64)
        w_scales = const.tile([P, PASSES, D_OUT], U8, align_bytes=64)
        w_grouped = {}

        def weight_piece(i):
            g, bank = divmod(i, OUT_BANKS)
            cols = slice(bank * BANK, (bank + 1) * BANK)
            if bank == 0:
                grouped = const.tile([P, D_OUT, PACK], BF16, align_bytes=64, tag="w_grouped")
                w_grouped[g] = grouped
            nc.vector.tensor_copy(
                out=w_grouped[g][:, cols, :].rearrange("p (c i) t -> p c t i", i=4),
                in_=w_sb[:, g * PACK : (g + 1) * PACK, cols].rearrange("p t (c i) -> p c t i", i=4),
            )
            if bank == OUT_BANKS - 1:
                nc.vector.quantize_mx(
                    out=w_codes[:, g, :].bitcast(FP8X4),
                    scales=w_scales[:, g, :],
                    in_=w_grouped[g][:].rearrange("p n t -> p (n t)"),
                )

        gates = {}

        def gate_piece(pair, j):
            grp, g = divmod(pair, PASSES)
            if j == 0:
                gate = gate_pool.tile([P, ROW_TILES, P, PACK], F32)
                gates[pair] = gate
            u_ps = ps_ring.tile([P, PACK, P], F32, tag="ring")
            for t in range(PACK):
                c = g * PACK + t
                nc.tensor.matmul(
                    out=u_ps[:, t, :],
                    lhsT=wg_sb[:, c * P : (c + 1) * P],
                    rhs=g_t[:, grp, j, :],
                    start=True,
                    stop=True,
                )
            nc.scalar.activation(
                out=gates[pair][:, j, :, :], in_=u_ps[:].rearrange("p t n -> p n t"), func=ACT.Sigmoid
            )

        q_t = {}

        def q_piece(r, half):
            grp, j = divmod(r, ROW_TILES)
            if half == 0:
                words = qt_pool.tile([P, HEADS, P], F32)
                q_t[r] = words
            tq_ps = ps_ring.tile([P, HEADS_PER_BANK, P], F32, tag="ring")
            for hh in range(HEADS_PER_BANK):
                h = half * HEADS_PER_BANK + hh
                nc.tensor.transpose(tq_ps[:, hh, :], q_tiles[grp][:, h, j, :].bitcast(F32), ident_f32[:])
            heads = slice(half * HEADS_PER_BANK, (half + 1) * HEADS_PER_BANK)
            nc.scalar.copy(out=q_t[r][:, heads, :], in_=tq_ps[:])

        o_banks = {}

        def heads_piece(r, half):
            b = r // (ROW_TILES * GROUPS_PER_SEQ)
            o_ps = ps_o.tile([P, HEADS_PER_BANK, HEAD_DIM], F32)
            o_banks[(r, half)] = o_ps
            for hh in range(HEADS_PER_BANK):
                h = half * HEADS_PER_BANK + hh
                pairs = q_t[r][:, h, :].bitcast(BF16).rearrange("w (n e) -> w n e", e=2)
                for e in range(2):
                    nc.tensor.matmul(
                        out=o_ps[:, hh, :],
                        lhsT=pairs[:, :, e],
                        rhs=kv_sb[:, b * HEADS + h, e, :],
                        start=(e == 0),
                        stop=(e == 1),
                    )

        x_rows = {}

        def drain_piece(r, half):
            grp, j = divmod(r, ROW_TILES)
            if j == 0 and half == 0:
                o_rows = x_pool.tile([P, ROW_TILES, INNER], F32)
                x_rows[grp] = o_rows
            nc.scalar.copy(
                out=x_rows[grp][:, j, half * BANK : (half + 1) * BANK],
                in_=o_banks[(r, half)][:].rearrange("p h d -> p (h d)"),
            )

        stats_of = {}

        def stats_piece(r):
            grp, j = divmod(r, ROW_TILES)
            stats = stat_pool.tile([P, O_BANKS, 6], F32)
            for half in range(O_BANKS):
                nc.vector.bn_stats(
                    out=stats[:, half, :], in_=x_rows[grp][:, j, half * BANK : (half + 1) * BANK]
                )
            stats_of[r] = stats

        def norm_piece(r):
            grp, j = divmod(r, ROW_TILES)
            mean_var = stat_pool.tile([P, 2], F32)
            nc.vector.bn_aggr(out=mean_var[:], in_=stats_of[r][:].rearrange("p a s -> p (a s)"))
            var_eps = stat_pool.tile([P, 1], F32)
            nc.vector.tensor_scalar(
                out=var_eps[:], in0=mean_var[:, 1:2], scalar1=LN_EPS, scalar2=None, op0=ALU.add
            )
            neg_mean = stat_pool.tile([P, 1], F32)
            nc.vector.tensor_scalar(
                out=neg_mean[:], in0=mean_var[:, 0:1], scalar1=-1.0, scalar2=None, op0=ALU.mult
            )
            rstd = stat_pool.tile([P, 1], F32)
            nc.gpsimd.tensor_tensor(out=rstd[:], in0=var_eps[:], in1=neg_half[:], op=ALU.pow)
            nc.gpsimd.tensor_scalar(
                out=x_rows[grp][:, j, :],
                in0=x_rows[grp][:, j, :],
                scalar1=neg_mean[:, 0:1],
                scalar2=rstd[:, 0:1],
                op0=ALU.add,
                op1=ALU.mult,
            )

        y_t = {}

        def flip_piece(pair, step):
            grp, g = divmod(pair, PASSES)
            if step == 0:
                scaled = y_pool.tile([P, PACK, ROW_TILES, P], F32)
                y_t[pair] = scaled
            xt_ps = ps_ring.tile([P, CHUNKS_PER_BANK, ROW_TILES, P], F32, tag="ring")
            for i in range(CHUNKS_PER_BANK):
                c = g * PACK + step * CHUNKS_PER_BANK + i
                for j in range(ROW_TILES):
                    nc.tensor.transpose(
                        xt_ps[:, i, j, :], x_rows[grp][:, j, c * P : (c + 1) * P], ident_f32[:]
                    )
            for i in range(CHUNKS_PER_BANK):
                t = step * CHUNKS_PER_BANK + i
                c = g * PACK + t
                nc.scalar.activation(
                    out=y_t[pair][:, t, :, :],
                    in_=xt_ps[:, i, :, :],
                    func=ACT.Identity,
                    scale=gamma_beta[:, c : c + 1],
                    bias=gamma_beta[:, CHUNKS + c : CHUNKS + c + 1],
                )

        h_bf = {}
        h_mx = {}

        def product_piece(pair):
            h_grouped = y_pool.tile([P, GROUP, PACK], BF16, align_bytes=64)
            nc.vector.tensor_tensor(
                out=h_grouped[:],
                in0=y_t[pair][:].rearrange("p t j n -> p (j n) t"),
                in1=gates[pair][:].rearrange("p j n t -> p (j n) t"),
                op=ALU.mult,
            )
            h_bf[pair] = h_grouped

        def quantise_piece(pair):
            h_codes = mx_pool.tile([P, GROUP], U32, align_bytes=64)
            h_scales = mx_pool.tile([P, GROUP], U8, align_bytes=64)
            nc.vector.quantize_mx(
                out=h_codes[:].bitcast(FP8X4),
                scales=h_scales[:],
                in_=h_bf[pair][:].rearrange("p m t -> p (m t)"),
            )
            h_mx[pair] = (h_codes, h_scales)

        results = {}

        def project_piece(r, bank):
            grp, j = divmod(r, ROW_TILES)
            b, s = divmod(grp, GROUPS_PER_SEQ)
            rows = slice(j * P, (j + 1) * P)
            cols = slice(bank * BANK, (bank + 1) * BANK)
            if bank == 0:
                result = out_pool.tile([P, D_OUT], F32)
                results[r] = result
            acc = ps_acc.tile([P, BANK], F32)
            for g in range(PASSES):
                h_codes, h_scales = h_mx[grp * PASSES + g]
                nc.tensor.matmul_mx(
                    out=acc[:],
                    lhsT=h_codes[:, rows].bitcast(FP8X4),
                    lhsT_scale=h_scales[:, rows],
                    rhs=w_codes[:, g, cols].bitcast(FP8X4),
                    rhs_scale=w_scales[:, g, cols],
                    start=(g == 0),
                    stop=(g == PASSES - 1),
                )
            nc.vector.tensor_tensor(
                out=results[r][:, cols], in0=acc[:], in1=bias_bf[:, cols], op=ALU.add
            )
            if bank == OUT_BANKS - 1:
                out_rows = out[b, s * GROUP : (s + 1) * GROUP, :].rearrange(
                    "(p j) d -> p j d", j=ROW_TILES
                )
                nc.sync.dma_start(out=out_rows[:, j, :], in_=results[r][:])

        def run(piece, index, count, *step):
            if 0 <= index < count:
                piece(index, *step)

        for tick in range(-GATE_LEAD, ROWS + PROJECT_LAG):
            run(product_piece, tick - PRODUCT_LAG, PAIRS)
            run(stats_piece, tick - STATS_LAG, ROWS)
            run(quantise_piece, tick - PRODUCT_LAG, PAIRS)
            run(norm_piece, tick - STATS_LAG, ROWS)
            run(weight_piece, tick - W_TICK, PASSES * OUT_BANKS)
            run(flip_piece, tick - FLIP_LAG, PAIRS, 0)
            run(flip_piece, tick - FLIP_LAG, PAIRS, 1)
            run(heads_piece, tick, ROWS, 0)
            run(drain_piece, tick, ROWS, 0)
            run(q_piece, tick + Q_LEAD, ROWS, 0)
            run(q_piece, tick + Q_LEAD, ROWS, 1)
            run(heads_piece, tick, ROWS, 1)
            run(drain_piece, tick, ROWS, 1)
            run(gate_piece, tick + GATE_LEAD, PAIRS, 0)
            run(project_piece, tick - PROJECT_LAG, ROWS, 0)
            run(gate_piece, tick + GATE_LEAD, PAIRS, 1)
            run(project_piece, tick - PROJECT_LAG, ROWS, 1)
            grp, j = divmod(tick + Q_LEAD, ROW_TILES)
            if j == ROW_TILES - 1 and 0 <= grp < GROUPS - Q_BUFS:
                load_q(grp + Q_BUFS)
